import numpy as np
import ml_dtypes


def mxq(x, axis, fmt="e4m3"):
    dtype, down = {"e4m3": (ml_dtypes.float8_e4m3fn, 7), "e5m2": (ml_dtypes.float8_e5m2, 14)}[fmt]
    v = np.moveaxis(np.asarray(x, np.float32).astype(ml_dtypes.bfloat16).astype(np.float64), axis, -1)
    blocks = v.reshape(v.shape[:-1] + (-1, 32))
    amax = np.abs(blocks).max(-1, keepdims=True)
    byte = np.maximum(np.where(amax > 0, np.frexp(amax)[1] - 1 + 127, 0) - down, 1)
    scale = np.exp2(byte - 127.0)
    codes = (blocks / scale).astype(np.float32).astype(dtype).astype(np.float64)
    return np.moveaxis((codes * scale).reshape(v.shape), -1, axis)


WIDE = False


def mx_kscale(k):
    if not WIDE:
        return np.ones(k)
    levels = np.array([10, -10, 5, -5, 0])
    if k % 512:
        return np.exp2(np.random.permutation(np.resize(levels, k // 32))).repeat(32)
    a = np.empty((k // 512, 16))
    for p in range(k // 512):
        a[p, :8] = np.random.permutation(np.resize(levels, 8))
        for g in range(8):
            far = levels[np.abs(levels - a[p, g]) >= 10]
            a[p, g + 8] = far[np.random.randint(len(far))]
    return np.exp2(a.ravel()).repeat(32)


BF16 = ml_dtypes.bfloat16


def bf(x):
    return np.asarray(x, np.float32).astype(BF16)


def f64(x):
    return np.asarray(x).astype(np.float64)


B, I, H, L, P, G = 128, 1024, 1024, 4, 2, 4


def sigmoid(v):
    return 1.0 / (1.0 + np.exp(-v))


def setup_inputs():
    s = mx_kscale(I)
    return {"h_below": bf(np.random.standard_normal((B, I)) * 0.3 * s),
            "gates_rec": bf(np.random.standard_normal((B, G * H)) * 0.7),
            "c": bf(np.random.standard_normal((B, H))),
            "w_ih": bf(np.random.standard_normal((G * H, I)) * 1.5 / np.sqrt(I) / s),
            "b_ih": bf(np.random.standard_normal(G * H) * 0.3),
            "b_hh": bf(np.random.standard_normal(G * H) * 0.3)}


def reference(h_below, gates_rec, c, w_ih, b_ih, b_hh):
    gates = (mxq(f64(h_below), 1, "e4m3") @ mxq(f64(w_ih), 1, "e4m3").T) + f64(b_ih) + f64(gates_rec) + f64(b_hh)
    i, f, g, o = np.split(gates, G, axis=-1)
    c_new = sigmoid(f) * f64(c) + sigmoid(i) * np.tanh(g)
    h_new = sigmoid(o) * np.tanh(c_new)
    return h_new, c_new

@@ -1,0 +1,253 @@
+from contextlib import ExitStack
+
+import concourse.mybir as mybir
+from concourse.masks import make_identity
+
+F32 = mybir.dt.float32
+BF16 = mybir.dt.bfloat16
+U32 = mybir.dt.uint32
+U8 = mybir.dt.uint8
+FP8X4 = mybir.dt.float8_e4m3fn_x4
+ACT = mybir.ActivationFunctionType
+ALU = mybir.AluOpType
+
+P = 128
+FEATURES = 1024
+HIDDEN = 1024
+GATES = 4
+GATE_F, GATE_G, GATE_O = 1, 2, 3
+PACK = 4
+PASSES = FEATURES // (P * PACK)
+HALVES = 2
+WORDS = FEATURES // 2
+BANK = 512
+PARTS = HIDDEN // BANK
+SLABS = PARTS * GATES
+PIECES = 2
+ROWS = BANK // PIECES
+TILES = ROWS // P
+
+FLOPS = 2 * P * FEATURES * GATES * HIDDEN
+
+
+def tile_yourlstm_pc_kernel(tc, h_below, gates_rec, c_old, w_ih, b_ih, b_hh, out_0, out_1):
+    nc = tc.nc
+    with ExitStack() as ctx:
+        keep = ctx.enter_context(tc.tile_pool(name="keep", bufs=1))
+        w_pool = ctx.enter_context(tc.tile_pool(name="w", bufs=SLABS * PIECES))
+        quant = ctx.enter_context(tc.tile_pool(name="quant", bufs=2 * PIECES))
+        stage = ctx.enter_context(tc.tile_pool(name="stage", bufs=2))
+        active_pool = ctx.enter_context(tc.tile_pool(name="active", bufs=GATES))
+        psum_words = ctx.enter_context(tc.psum_pool(name="psum_words", bufs=3 * PASSES))
+        psum_gates = ctx.enter_context(tc.psum_pool(name="psum_gates", bufs=1))
+        psum_bias = ctx.enter_context(tc.psum_pool(name="psum_bias", bufs=1))
+        ctx.enter_context(tc.manual_schedule())
+
+        def gate_of(t):
+            return t % GATES
+
+        def part_of(t):
+            return t // GATES
+
+        def live(t):
+            return 0 <= t < SLABS
+
+        def units(part):
+            return slice(part * BANK, (part + 1) * BANK)
+
+        bias_blocks = GATES * HIDDEN // P
+        bias_rows = keep.tile([P, P], BF16)
+        nc.vector.memset(bias_rows[2 * bias_blocks : P, :], 0.0)
+        nc.scalar.dma_start(out=bias_rows[0:bias_blocks, :], in_=b_ih.rearrange("(m r) -> m r", r=P))
+        nc.scalar.dma_start(
+            out=bias_rows[bias_blocks : 2 * bias_blocks, :], in_=b_hh.rearrange("(m r) -> m r", r=P)
+        )
+
+        h_rows = keep.tile([P, FEATURES], BF16)
+        nc.sync.dma_start(out=h_rows[:], in_=h_below)
+        w_pieces = w_ih.rearrange("(g v e x r) k -> g v e r x k", g=GATES, v=PARTS, e=PIECES, r=P)
+        rec_parts = gates_rec.rearrange("b (g v y) -> v b g y", g=GATES, v=PARTS)
+        w_rows = {}
+        rec_rows = {}
+        c_rows = keep.tile([P, HIDDEN], BF16)
+        for t in range(SLABS):
+            for e in range(PIECES):
+                w_rows[(t, e)] = w_pool.tile([P, TILES * FEATURES], BF16, name="w_rows", tag="w_rows")
+                nc.sync.dma_start(
+                    out=w_rows[(t, e)][:].rearrange("r (x k) -> r x k", x=TILES),
+                    in_=w_pieces[gate_of(t), part_of(t), e],
+                )
+            if gate_of(t) == 1:
+                rec_rows[part_of(t)] = keep.tile([P, GATES, BANK], BF16, name="rec_rows%d" % part_of(t))
+                nc.sync.dma_start(out=rec_rows[part_of(t)][:], in_=rec_parts[part_of(t)])
+            if t == GATE_F + 2:
+                nc.sync.dma_start(out=c_rows[:], in_=c_old)
+
+        ident_f32 = keep.tile([P, P], F32)
+        make_identity(nc, ident_f32[:])
+        ident_bf16 = keep.tile([P, P], BF16)
+        nc.vector.tensor_copy(out=ident_bf16[:], in_=ident_f32[:])
+        warm = keep.tile([P, 1], F32)
+        nc.vector.memset(warm[:], 0.0)
+        warm_out = keep.tile([P, 1], F32)
+        nc.scalar.activation(out=warm_out[:], in_=warm[:], func=ACT.Sigmoid)
+
+        h_words = h_rows[:].bitcast(F32)
+        h_t = psum_bias.tile([P, PASSES, HALVES, P], F32, tag="bias_bank")
+        for s in range(PASSES):
+            for u in range(HALVES):
+                first = s * HALVES * P
+                nc.tensor.transpose(
+                    h_t[:, s, u, :], h_words[:, first + u : first + HALVES * P : HALVES], ident_f32[:]
+                )
+        h_grouped = keep.tile([P, PASSES * P * PACK], BF16, align_bytes=64)
+        nc.vector.tensor_copy(
+            out=h_grouped[:].bitcast(F32).rearrange("q (s m u) -> q s m u", s=PASSES, u=HALVES),
+            in_=h_t[:].rearrange("q s u m -> q s m u"),
+        )
+
+        bias_col = keep.tile([P, bias_blocks], F32)
+
+        def transpose_biases():
+            bias_t = psum_bias.tile([P, P], BF16, tag="bias_bank")
+            nc.tensor.transpose(bias_t[:], bias_rows[:], ident_bf16[:])
+            bias_both = keep.tile([P, 2 * bias_blocks], F32)
+            nc.vector.tensor_copy(out=bias_both[:], in_=bias_t[:, 0 : 2 * bias_blocks])
+            nc.vector.tensor_add(
+                out=bias_col[:], in0=bias_both[:, 0:bias_blocks], in1=bias_both[:, bias_blocks : 2 * bias_blocks]
+            )
+
+        h_codes = keep.tile([P, PASSES * P], U32, align_bytes=64)
+        h_scales = keep.tile([P, PASSES * P], U8, align_bytes=64)
+        nc.vector.quantize_mx(out=h_codes[:].bitcast(FP8X4), scales=h_scales[:], in_=h_grouped[:])
+
+        c_new = keep.tile([P, HIDDEN], F32)
+        h_new = keep.tile([P, HIDDEN], F32)
+        bias_banks = {}
+        rest = {}
+        word_banks = {}
+        grouped = {}
+        codes = {}
+        scales = {}
+        products = {}
+        gates = {}
+        active = {}
+        kept = {}
+        fresh = {}
+        tanh_c = {}
+
+        def broadcast_bias(t):
+            bias_banks[t] = psum_bias.tile([P, BANK // P, P], F32, name="bias_bank", tag="bias_bank")
+            for x in range(BANK // P):
+                m = (gate_of(t) * HIDDEN + part_of(t) * BANK) // P + x
+                nc.tensor.transpose(
+                    bias_banks[t][:, x, :], bias_col[:, m : m + 1].to_broadcast([P, P]), ident_f32[:]
+                )
+
+        def add_bias_to_rec(t):
+            rest[t] = stage.tile([P, BANK], F32, name="rest", tag="rest")
+            nc.vector.tensor_tensor(
+                out=rest[t][:],
+                in0=bias_banks[t][:].rearrange("b x r -> b (x r)"),
+                in1=rec_rows[part_of(t)][:, gate_of(t), :],
+                op=ALU.add,
+            )
+
+        def transpose_w(t):
+            for e in range(PIECES):
+                words = w_rows[(t, e)][:].bitcast(F32)
+                for s in range(PASSES):
+                    bank = psum_words.tile([P, TILES, HALVES, P], F32, name="word_bank", tag="word_bank")
+                    for x in range(TILES):
+                        for u in range(HALVES):
+                            first = x * WORDS + s * HALVES * P
+                            nc.tensor.transpose(
+                                bank[:, x, u, :], words[:, first + u : first + HALVES * P : HALVES], ident_f32[:]
+                            )
+                    word_banks[(t, e, s)] = bank
+
+        def regroup(t, e):
+            grouped[(t, e)] = quant.tile([P, PASSES * ROWS * PACK], BF16, name="grouped", tag="grouped", align_bytes=64)
+            words = grouped[(t, e)][:].bitcast(F32)
+            for s in range(PASSES):
+                nc.scalar.copy(
+                    out=words[:, s * BANK : (s + 1) * BANK].rearrange("q (x r u) -> q x r u", x=TILES, u=HALVES),
+                    in_=word_banks[(t, e, s)][:].rearrange("q x u r -> q x r u"),
+                )
+
+        def quantise(t, e):
+            codes[(t, e)] = quant.tile([P, PASSES * ROWS], U32, name="codes", tag="codes", align_bytes=64)
+            scales[(t, e)] = quant.tile([P, PASSES * ROWS], U8, name="scales", tag="scales", align_bytes=64)
+            nc.vector.quantize_mx(
+                out=codes[(t, e)][:].bitcast(FP8X4), scales=scales[(t, e)][:], in_=grouped[(t, e)][:]
+            )
+
+        def multiply(t):
+            products[t] = psum_gates.tile([P, BANK], F32, name="product", tag="product")
+            for e in range(PIECES):
+                for s in range(PASSES):
+                    nc.tensor.matmul_mx(
+                        out=products[t][:, e * ROWS : (e + 1) * ROWS],
+                        lhsT=h_codes[:, s * P : (s + 1) * P].bitcast(FP8X4),
+                        lhsT_scale=h_scales[:, s * P : (s + 1) * P],
+                        rhs=codes[(t, e)][:, s * ROWS : (s + 1) * ROWS].bitcast(FP8X4),
+                        rhs_scale=scales[(t, e)][:, s * ROWS : (s + 1) * ROWS],
+                        start=(s == 0),
+                        stop=(s == PASSES - 1),
+                    )
+
+        def add_rest(t):
+            gates[t] = stage.tile([P, BANK], F32, name="gates", tag="gates")
+            nc.vector.tensor_tensor(out=gates[t][:], in0=products[t][:], in1=rest[t][:], op=ALU.add)
+
+        def activate(t):
+            active[t] = active_pool.tile([P, BANK], F32, name="active", tag="active")
+            func = ACT.Tanh if gate_of(t) == GATE_G else ACT.Sigmoid
+            nc.scalar.activation(out=active[t][:], in_=gates[t][:], func=func)
+
+        def use_gate(t):
+            part = part_of(t)
+            if gate_of(t) == GATE_F:
+                kept[part] = stage.tile([P, BANK], F32, name="kept", tag="kept")
+                nc.vector.tensor_mul(out=kept[part][:], in0=active[t][:], in1=c_rows[:, units(part)])
+            if gate_of(t) == GATE_G:
+                fresh[part] = stage.tile([P, BANK], F32, name="fresh", tag="fresh")
+                nc.vector.tensor_mul(out=fresh[part][:], in0=active[t - GATE_G][:], in1=active[t][:])
+            if gate_of(t) == GATE_O:
+                nc.vector.tensor_mul(out=h_new[:, units(part)], in0=active[t][:], in1=tanh_c[part][:])
+                nc.sync.dma_start(out=out_0[:, units(part)], in_=h_new[:, units(part)])
+
+        def update_cell(part):
+            nc.vector.tensor_add(out=c_new[:, units(part)], in0=kept[part][:], in1=fresh[part][:])
+            nc.sync.dma_start(out=out_1[:, units(part)], in_=c_new[:, units(part)])
+
+        def activate_cell(part):
+            tanh_c[part] = stage.tile([P, BANK], F32, name="tanh_c", tag="tanh_c")
+            nc.scalar.activation(out=tanh_c[part][:], in_=c_new[:, units(part)], func=ACT.Tanh)
+
+        for t in range(SLABS + 2):
+            used = gate_of(t - 2) if live(t - 2) else None
+            if live(t):
+                transpose_w(t)
+            if live(t - 1):
+                broadcast_bias(t - 1)
+                multiply(t - 1)
+            if live(t):
+                regroup(t, 0)
+                quantise(t, 0)
+            if live(t - 1):
+                add_bias_to_rec(t - 1)
+            if used == GATE_O:
+                activate_cell(part_of(t - 2))
+            if live(t - 2):
+                activate(t - 2)
+                use_gate(t - 2)
+            if used == GATE_G:
+                update_cell(part_of(t - 2))
+            if live(t - 1):
+                add_rest(t - 1)
+            if live(t):
+                regroup(t, 1)
+                quantise(t, 1)
+            if t == 0:
+                transpose_biases()

@@ -65,7 +65,7 @@ def tile_yourlstm_pc_kernel(tc, h_below, gates_rec, c_old, w_ih, b_ih, b_hh, out
 
         h_rows = keep.tile([P, FEATURES], BF16)
         nc.sync.dma_start(out=h_rows[:], in_=h_below)
-        w_pieces = w_ih.rearrange("(g v e x r) k -> g v e r x k", g=GATES, v=PARTS, e=PIECES, r=P)
+        w_pieces = w_ih.rearrange("(g v e r x) k -> g v e r x k", g=GATES, v=PARTS, e=PIECES, r=P)
         rec_parts = gates_rec.rearrange("b (g v y) -> v b g y", g=GATES, v=PARTS)
         w_rows = {}
         rec_rows = {}
@@ -171,8 +171,8 @@ def tile_yourlstm_pc_kernel(tc, h_below, gates_rec, c_old, w_ih, b_ih, b_hh, out
             words = grouped[(t, e)][:].bitcast(F32)
             for s in range(PASSES):
                 nc.scalar.copy(
-                    out=words[:, s * BANK : (s + 1) * BANK].rearrange("q (x r u) -> q x r u", x=TILES, u=HALVES),
-                    in_=word_banks[(t, e, s)][:].rearrange("q x u r -> q x r u"),
+                    out=words[:, s * BANK : (s + 1) * BANK].rearrange("q (r x u) -> q r x u", x=TILES, u=HALVES),
+                    in_=word_banks[(t, e, s)][:].rearrange("q x u r -> q r x u"),
                 )
 
         def quantise(t, e):

@@ -26,6 +26,19 @@ SLABS = PARTS * GATES
 PIECES = 2
 ROWS = BANK // PIECES
 TILES = ROWS // P
+STEPS = SLABS * PIECES
+BUSY = 1024
+FIRST = 1536
+SECOND = 1024
+SUM_FROM = 2
+FILLER = 256
+LAG = 2
+REC_AT = (0, 2)
+C_AT = 1
+NB = 2
+WB = 5
+PB = 2
+BB = 1
 
 FLOPS = 2 * P * FEATURES * GATES * HIDDEN
 
@@ -35,19 +48,19 @@ def tile_yourlstm_pc_kernel(tc, h_below, gates_rec, c_old, w_ih, b_ih, b_hh, out
     with ExitStack() as ctx:
         keep = ctx.enter_context(tc.tile_pool(name="keep", bufs=1))
         w_pool = ctx.enter_context(tc.tile_pool(name="w", bufs=SLABS * PIECES))
-        quant = ctx.enter_context(tc.tile_pool(name="quant", bufs=2 * PIECES))
-        stage = ctx.enter_context(tc.tile_pool(name="stage", bufs=2))
+        quant = ctx.enter_context(tc.tile_pool(name="quant", bufs=3 * PIECES))
+        stage = ctx.enter_context(tc.tile_pool(name="stage", bufs=NB))
         active_pool = ctx.enter_context(tc.tile_pool(name="active", bufs=GATES))
-        psum_words = ctx.enter_context(tc.psum_pool(name="psum_words", bufs=3 * PASSES))
-        psum_gates = ctx.enter_context(tc.psum_pool(name="psum_gates", bufs=1))
-        psum_bias = ctx.enter_context(tc.psum_pool(name="psum_bias", bufs=1))
+        psum_words = ctx.enter_context(tc.psum_pool(name="psum_words", bufs=WB))
+        psum_gates = ctx.enter_context(tc.psum_pool(name="psum_gates", bufs=PB))
+        psum_bias = ctx.enter_context(tc.psum_pool(name="psum_bias", bufs=BB))
         ctx.enter_context(tc.manual_schedule())
 
         def gate_of(t):
-            return t % GATES
+            return t % GATE_O if t < PARTS * GATE_O else GATE_O
 
         def part_of(t):
-            return t // GATES
+            return t // GATE_O if t < PARTS * GATE_O else t - PARTS * GATE_O
 
         def live(t):
             return 0 <= t < SLABS
@@ -57,6 +70,11 @@ def tile_yourlstm_pc_kernel(tc, h_below, gates_rec, c_old, w_ih, b_ih, b_hh, out
 
         bias_blocks = GATES * HIDDEN // P
         bias_rows = keep.tile([P, P], BF16)
+        filler_in = keep.tile([P, FILLER * PACK], BF16, align_bytes=64)
+        filler_codes = keep.tile([P, FILLER], U32, align_bytes=64)
+        filler_scales = keep.tile([P, FILLER], U8, align_bytes=64)
+        nc.vector.memset(filler_in[:], 1.0)
+        nc.vector.quantize_mx(out=filler_codes[:].bitcast(FP8X4), scales=filler_scales[:], in_=filler_in[:])
         nc.vector.memset(bias_rows[2 * bias_blocks : P, :], 0.0)
         nc.scalar.dma_start(out=bias_rows[0:bias_blocks, :], in_=b_ih.rearrange("(m r) -> m r", r=P))
         nc.scalar.dma_start(
@@ -73,53 +91,32 @@ def tile_yourlstm_pc_kernel(tc, h_below, gates_rec, c_old, w_ih, b_ih, b_hh, out
         for t in range(SLABS):
             for e in range(PIECES):
                 w_rows[(t, e)] = w_pool.tile([P, TILES * FEATURES], BF16, name="w_rows", tag="w_rows")
-                nc.sync.dma_start(
-                    out=w_rows[(t, e)][:].rearrange("r (x k) -> r x k", x=TILES),
-                    in_=w_pieces[gate_of(t), part_of(t), e],
-                )
-            if gate_of(t) == 1:
-                rec_rows[part_of(t)] = keep.tile([P, GATES, BANK], BF16, name="rec_rows%d" % part_of(t))
-                nc.sync.dma_start(out=rec_rows[part_of(t)][:], in_=rec_parts[part_of(t)])
-            if t == GATE_F + 2:
+                piece_rows = w_rows[(t, e)][:].rearrange("r (x k) -> r x k", x=TILES)
+                source = w_pieces[gate_of(t), part_of(t), e]
+                if (t, e) == (0, 0):
+                    for x in range(TILES):
+                        nc.sync.dma_start(out=piece_rows[:, x], in_=source[:, x])
+                else:
+                    nc.sync.dma_start(out=piece_rows, in_=source)
+            if t in REC_AT:
+                part = REC_AT.index(t)
+                rec_rows[part] = keep.tile([P, GATES, BANK], BF16, name="rec_rows%d" % part)
+                nc.sync.dma_start(out=rec_rows[part][:], in_=rec_parts[part])
+            if t == C_AT:
                 nc.sync.dma_start(out=c_rows[:], in_=c_old)
 
         ident_f32 = keep.tile([P, P], F32)
         make_identity(nc, ident_f32[:])
         ident_bf16 = keep.tile([P, P], BF16)
         nc.vector.tensor_copy(out=ident_bf16[:], in_=ident_f32[:])
+        sel = keep.tile([P, bias_blocks], BF16)
+        nc.vector.tensor_add(
+            out=sel[:], in0=ident_bf16[:, 0:bias_blocks], in1=ident_bf16[:, bias_blocks : 2 * bias_blocks]
+        )
         warm = keep.tile([P, 1], F32)
         nc.vector.memset(warm[:], 0.0)
         warm_out = keep.tile([P, 1], F32)
         nc.scalar.activation(out=warm_out[:], in_=warm[:], func=ACT.Sigmoid)
-
-        h_words = h_rows[:].bitcast(F32)
-        h_t = psum_bias.tile([P, PASSES, HALVES, P], F32, tag="bias_bank")
-        for s in range(PASSES):
-            for u in range(HALVES):
-                first = s * HALVES * P
-                nc.tensor.transpose(
-                    h_t[:, s, u, :], h_words[:, first + u : first + HALVES * P : HALVES], ident_f32[:]
-                )
-        h_grouped = keep.tile([P, PASSES * P * PACK], BF16, align_bytes=64)
-        nc.vector.tensor_copy(
-            out=h_grouped[:].bitcast(F32).rearrange("q (s m u) -> q s m u", s=PASSES, u=HALVES),
-            in_=h_t[:].rearrange("q s u m -> q s m u"),
-        )
-
-        bias_col = keep.tile([P, bias_blocks], F32)
-
-        def transpose_biases():
-            bias_t = psum_bias.tile([P, P], BF16, tag="bias_bank")
-            nc.tensor.transpose(bias_t[:], bias_rows[:], ident_bf16[:])
-            bias_both = keep.tile([P, 2 * bias_blocks], F32)
-            nc.vector.tensor_copy(out=bias_both[:], in_=bias_t[:, 0 : 2 * bias_blocks])
-            nc.vector.tensor_add(
-                out=bias_col[:], in0=bias_both[:, 0:bias_blocks], in1=bias_both[:, bias_blocks : 2 * bias_blocks]
-            )
-
-        h_codes = keep.tile([P, PASSES * P], U32, align_bytes=64)
-        h_scales = keep.tile([P, PASSES * P], U8, align_bytes=64)
-        nc.vector.quantize_mx(out=h_codes[:].bitcast(FP8X4), scales=h_scales[:], in_=h_grouped[:])
 
         c_new = keep.tile([P, HIDDEN], F32)
         h_new = keep.tile([P, HIDDEN], F32)
@@ -136,13 +133,81 @@ def tile_yourlstm_pc_kernel(tc, h_below, gates_rec, c_old, w_ih, b_ih, b_hh, out
         fresh = {}
         tanh_c = {}
 
-        def broadcast_bias(t):
-            bias_banks[t] = psum_bias.tile([P, BANK // P, P], F32, name="bias_bank", tag="bias_bank")
+        def piece(e):
+            return slice(e * ROWS, (e + 1) * ROWS)
+
+        def product_piece(h):
+            t, e = divmod(h, PIECES)
+            if t not in products:
+                products[t] = psum_gates.tile([P, BANK], F32, name="product", tag="product")
+            return products[t][:, piece(e)]
+
+        def mx_pass(out, lhs, lhs_scale, rhs, rhs_scale, start, stop):
+            nc.tensor.matmul_mx(
+                out=out, lhsT=lhs.bitcast(FP8X4), lhsT_scale=lhs_scale, rhs=rhs.bitcast(FP8X4), rhs_scale=rhs_scale,
+                start=start, stop=stop,
+            )
+
+        def multiply(h):
+            t, e = divmod(h, PIECES)
+            for s in range(PASSES):
+                mx_pass(
+                    product_piece(h), h_codes[:, s * P : (s + 1) * P], h_scales[:, s * P : (s + 1) * P],
+                    codes[(t, e)][:, s * ROWS : (s + 1) * ROWS], scales[(t, e)][:, s * ROWS : (s + 1) * ROWS],
+                    s == 0, s == PASSES - 1,
+                )
+
+        def fill(h, columns):
+            for i in range(columns // FILLER):
+                mx_pass(
+                    product_piece(h), filler_codes[:, 0:P], filler_scales[:, 0:P], filler_codes[:],
+                    filler_scales[:], True, True,
+                )
+
+        def spread_biases(t):
+            if t == 1:
+                bias_banks[t] = psum_gates.tile([P, BANK // P, P], F32, name="product", tag="product")
+            else:
+                bias_banks[t] = psum_bias.tile([P, BANK // P, P], F32, name="bias_bank", tag="bias_bank")
             for x in range(BANK // P):
                 m = (gate_of(t) * HIDDEN + part_of(t) * BANK) // P + x
-                nc.tensor.transpose(
-                    bias_banks[t][:, x, :], bias_col[:, m : m + 1].to_broadcast([P, P]), ident_f32[:]
-                )
+                if t < SUM_FROM:
+                    nc.tensor.transpose(bias_banks[t][:, x, :], bias_col[:, m : m + 1].to_broadcast([P, P]), ident_f32[:])
+                else:
+                    nc.tensor.matmul(
+                        bias_banks[t][:, x, :], sel[:, m : m + 1].to_broadcast([P, P]), bias_rows[:], start=True, stop=True
+                    )
+
+        def transpose(out, in_):
+            nc.tensor.transpose(out, in_, ident_f32[:])
+
+        fill(0, FIRST)
+        h_words = h_rows[:].bitcast(F32)
+        h_t = psum_bias.tile([P, PASSES, HALVES, P], F32, tag="bias_bank")
+        for s in range(PASSES):
+            for u in range(HALVES):
+                first = s * HALVES * P
+                transpose(h_t[:, s, u, :], h_words[:, first + u : first + HALVES * P : HALVES])
+        h_grouped = keep.tile([P, PASSES * P * PACK], BF16, align_bytes=64)
+        nc.vector.tensor_copy(
+            out=h_grouped[:].bitcast(F32).rearrange("q (s m u) -> q s m u", s=PASSES, u=HALVES),
+            in_=h_t[:].rearrange("q s u m -> q s m u"),
+        )
+        h_codes = keep.tile([P, PASSES * P], U32, align_bytes=64)
+        h_scales = keep.tile([P, PASSES * P], U8, align_bytes=64)
+        nc.vector.quantize_mx(out=h_codes[:].bitcast(FP8X4), scales=h_scales[:], in_=h_grouped[:])
+
+        fill(0, SECOND)
+        bias_col = keep.tile([P, bias_blocks], F32)
+
+        def transpose_biases():
+            bias_t = psum_bias.tile([P, P], BF16, tag="bias_bank")
+            nc.tensor.transpose(bias_t[:], bias_rows[:], ident_bf16[:])
+            bias_both = keep.tile([P, 2 * bias_blocks], F32)
+            nc.vector.tensor_copy(out=bias_both[:], in_=bias_t[:, 0 : 2 * bias_blocks])
+            nc.vector.tensor_add(
+                out=bias_col[:], in0=bias_both[:, 0:bias_blocks], in1=bias_both[:, bias_blocks : 2 * bias_blocks]
+            )
 
         def add_bias_to_rec(t):
             rest[t] = stage.tile([P, BANK], F32, name="rest", tag="rest")
@@ -153,57 +218,50 @@ def tile_yourlstm_pc_kernel(tc, h_below, gates_rec, c_old, w_ih, b_ih, b_hh, out
                 op=ALU.add,
             )
 
-        def transpose_w(t):
-            for e in range(PIECES):
-                words = w_rows[(t, e)][:].bitcast(F32)
-                for s in range(PASSES):
-                    bank = psum_words.tile([P, TILES, HALVES, P], F32, name="word_bank", tag="word_bank")
-                    for x in range(TILES):
-                        for u in range(HALVES):
-                            first = x * WORDS + s * HALVES * P
-                            nc.tensor.transpose(
-                                bank[:, x, u, :], words[:, first + u : first + HALVES * P : HALVES], ident_f32[:]
-                            )
-                    word_banks[(t, e, s)] = bank
+        def transpose_w(t, e, s, x):
+            if (t, e, s) not in word_banks:
+                word_banks[(t, e, s)] = psum_words.tile([P, TILES, HALVES, P], F32, name="word_bank", tag="word_bank")
+            words = w_rows[(t, e)][:].bitcast(F32)
+            for u in range(HALVES):
+                first = x * WORDS + s * HALVES * P
+                transpose(word_banks[(t, e, s)][:, x, u, :], words[:, first + u : first + HALVES * P : HALVES])
 
-        def regroup(t, e):
-            grouped[(t, e)] = quant.tile([P, PASSES * ROWS * PACK], BF16, name="grouped", tag="grouped", align_bytes=64)
-            words = grouped[(t, e)][:].bitcast(F32)
-            for s in range(PASSES):
-                nc.scalar.copy(
-                    out=words[:, s * BANK : (s + 1) * BANK].rearrange("q (r x u) -> q r x u", x=TILES, u=HALVES),
-                    in_=word_banks[(t, e, s)][:].rearrange("q x u r -> q r x u"),
+        def regroup(t, e, s):
+            if s == 0:
+                grouped[(t, e)] = quant.tile(
+                    [P, PASSES * ROWS * PACK], BF16, name="grouped", tag="grouped", align_bytes=64
                 )
-
-        def quantise(t, e):
-            codes[(t, e)] = quant.tile([P, PASSES * ROWS], U32, name="codes", tag="codes", align_bytes=64)
-            scales[(t, e)] = quant.tile([P, PASSES * ROWS], U8, name="scales", tag="scales", align_bytes=64)
-            nc.vector.quantize_mx(
-                out=codes[(t, e)][:].bitcast(FP8X4), scales=scales[(t, e)][:], in_=grouped[(t, e)][:]
+            words = grouped[(t, e)][:].bitcast(F32)
+            nc.scalar.copy(
+                out=words[:, s * BANK : (s + 1) * BANK].rearrange("q (r x u) -> q r x u", x=TILES, u=HALVES),
+                in_=word_banks[(t, e, s)][:].rearrange("q x u r -> q r x u"),
             )
 
-        def multiply(t):
-            products[t] = psum_gates.tile([P, BANK], F32, name="product", tag="product")
-            for e in range(PIECES):
-                for s in range(PASSES):
-                    nc.tensor.matmul_mx(
-                        out=products[t][:, e * ROWS : (e + 1) * ROWS],
-                        lhsT=h_codes[:, s * P : (s + 1) * P].bitcast(FP8X4),
-                        lhsT_scale=h_scales[:, s * P : (s + 1) * P],
-                        rhs=codes[(t, e)][:, s * ROWS : (s + 1) * ROWS].bitcast(FP8X4),
-                        rhs_scale=scales[(t, e)][:, s * ROWS : (s + 1) * ROWS],
-                        start=(s == 0),
-                        stop=(s == PASSES - 1),
-                    )
+        def quantise(t, e, first, last):
+            if first == 0:
+                codes[(t, e)] = quant.tile([P, PASSES * ROWS], U32, name="codes", tag="codes", align_bytes=64)
+                scales[(t, e)] = quant.tile([P, PASSES * ROWS], U8, name="scales", tag="scales", align_bytes=64)
+            cols = slice(first * ROWS, last * ROWS)
+            nc.vector.quantize_mx(
+                out=codes[(t, e)][:, cols].bitcast(FP8X4), scales=scales[(t, e)][:, cols],
+                in_=grouped[(t, e)][:, first * ROWS * PACK : last * ROWS * PACK],
+            )
 
-        def add_rest(t):
-            gates[t] = stage.tile([P, BANK], F32, name="gates", tag="gates")
-            nc.vector.tensor_tensor(out=gates[t][:], in0=products[t][:], in1=rest[t][:], op=ALU.add)
+        def add_rest(t, cols):
+            if cols.start == 0:
+                gates[t] = stage.tile([P, BANK], F32, name="gates", tag="gates")
+                active[t] = active_pool.tile([P, BANK], F32, name="active", tag="active")
+            nc.vector.tensor_tensor(out=gates[t][:, cols], in0=products[t][:, cols], in1=rest[t][:, cols], op=ALU.add)
 
-        def activate(t):
-            active[t] = active_pool.tile([P, BANK], F32, name="active", tag="active")
+        def activate(t, cols):
             func = ACT.Tanh if gate_of(t) == GATE_G else ACT.Sigmoid
-            nc.scalar.activation(out=active[t][:], in_=gates[t][:], func=func)
+            nc.scalar.activation(out=active[t][:, cols], in_=gates[t][:, cols], func=func)
+
+        def emit_hidden(t, cols):
+            part = part_of(t)
+            out_cols = slice(part * BANK + cols.start, part * BANK + cols.stop)
+            nc.vector.tensor_mul(out=h_new[:, out_cols], in0=active[t][:, cols], in1=tanh_c[part][:, cols])
+            nc.sync.dma_start(out=out_0[:, out_cols], in_=h_new[:, out_cols])
 
         def use_gate(t):
             part = part_of(t)
@@ -213,41 +271,63 @@ def tile_yourlstm_pc_kernel(tc, h_below, gates_rec, c_old, w_ih, b_ih, b_hh, out
             if gate_of(t) == GATE_G:
                 fresh[part] = stage.tile([P, BANK], F32, name="fresh", tag="fresh")
                 nc.vector.tensor_mul(out=fresh[part][:], in0=active[t - GATE_G][:], in1=active[t][:])
+                nc.vector.tensor_add(out=c_new[:, units(part)], in0=kept[part][:], in1=fresh[part][:])
+                nc.sync.dma_start(out=out_1[:, units(part)], in_=c_new[:, units(part)])
             if gate_of(t) == GATE_O:
-                nc.vector.tensor_mul(out=h_new[:, units(part)], in0=active[t][:], in1=tanh_c[part][:])
-                nc.sync.dma_start(out=out_0[:, units(part)], in_=h_new[:, units(part)])
-
-        def update_cell(part):
-            nc.vector.tensor_add(out=c_new[:, units(part)], in0=kept[part][:], in1=fresh[part][:])
-            nc.sync.dma_start(out=out_1[:, units(part)], in_=c_new[:, units(part)])
+                emit_hidden(t, WHOLE)
 
         def activate_cell(part):
             tanh_c[part] = stage.tile([P, BANK], F32, name="tanh_c", tag="tanh_c")
             nc.scalar.activation(out=tanh_c[part][:], in_=c_new[:, units(part)], func=ACT.Tanh)
 
-        for t in range(SLABS + 2):
-            used = gate_of(t - 2) if live(t - 2) else None
-            if live(t):
-                transpose_w(t)
-            if live(t - 1):
-                broadcast_bias(t - 1)
-                multiply(t - 1)
-            if live(t):
-                regroup(t, 0)
-                quantise(t, 0)
-            if live(t - 1):
-                add_bias_to_rec(t - 1)
-            if used == GATE_O:
-                activate_cell(part_of(t - 2))
-            if live(t - 2):
-                activate(t - 2)
-                use_gate(t - 2)
-            if used == GATE_G:
-                update_cell(part_of(t - 2))
-            if live(t - 1):
-                add_rest(t - 1)
-            if live(t):
-                regroup(t, 1)
-                quantise(t, 1)
-            if t == 0:
+        WHOLE = slice(0, BANK)
+        for h in range(STEPS):
+            t, e = divmod(h, PIECES)
+            if h >= 3 and e == 0:
+                add_bias_to_rec(t)
+            for i in range(PASSES * TILES):
+                s, x = divmod(i, TILES) if h else divmod(i, PASSES)[::-1]
+                transpose_w(t, e, s, x)
+            if h == 0:
                 transpose_biases()
+            done = 0
+            if h >= LAG:
+                multiply(h - LAG)
+                done += PASSES * ROWS
+            if e == 1 and SUM_FROM <= t + 1 < SLABS:
+                spread_biases(t + 1)
+                done += BANK
+            if h < STEPS - 1:
+                fill(max(h - LAG + 1, 0), BUSY - done)
+            if h == 0:
+                spread_biases(0)
+                spread_biases(1)
+                fill(0, BUSY)
+            for s in range(PASSES):
+                regroup(t, e, s)
+            if h == 2:
+                add_bias_to_rec(0)
+                add_bias_to_rec(1)
+            if e == 1:
+                if t >= 1:
+                    add_rest(t - 1, WHOLE)
+                if t >= 2 and gate_of(t - 2) == GATE_G:
+                    activate_cell(part_of(t - 2))
+            elif t >= 2:
+                activate(t - 2, WHOLE)
+            if h < STEPS - 1:
+                quantise(t, e, 0, PASSES)
+            if e == 0 and t >= 2:
+                use_gate(t - 2)
+        multiply(h - 1)
+        quantise(t, e, 0, 1)
+        activate(t - 1, WHOLE)
+        add_rest(t, piece(0))
+        activate(t, piece(0))
+        quantise(t, e, 1, 2)
+        multiply(h)
+        use_gate(t - 1)
+        add_rest(t, piece(1))
+        activate(t, piece(1))
+        for e in range(PIECES):
+            emit_hidden(t, piece(e))

@@ -27,18 +27,11 @@ PIECES = 2
 ROWS = BANK // PIECES
 TILES = ROWS // P
 STEPS = SLABS * PIECES
-BUSY = 1024
-FIRST = 1536
-SECOND = 1024
-SUM_FROM = 2
-FILLER = 256
+WHOLE = slice(0, BANK)
+TURNED = (0, 1)
 LAG = 2
-REC_AT = (0, 2)
-C_AT = 1
-NB = 2
-WB = 5
-PB = 2
-BB = 1
+REC_AT = (1, 3)
+C_AT = 2
 
 FLOPS = 2 * P * FEATURES * GATES * HIDDEN
 
@@ -49,11 +42,11 @@ def tile_yourlstm_pc_kernel(tc, h_below, gates_rec, c_old, w_ih, b_ih, b_hh, out
         keep = ctx.enter_context(tc.tile_pool(name="keep", bufs=1))
         w_pool = ctx.enter_context(tc.tile_pool(name="w", bufs=SLABS * PIECES))
         quant = ctx.enter_context(tc.tile_pool(name="quant", bufs=3 * PIECES))
-        stage = ctx.enter_context(tc.tile_pool(name="stage", bufs=NB))
+        stage = ctx.enter_context(tc.tile_pool(name="stage", bufs=2))
         active_pool = ctx.enter_context(tc.tile_pool(name="active", bufs=GATES))
-        psum_words = ctx.enter_context(tc.psum_pool(name="psum_words", bufs=WB))
-        psum_gates = ctx.enter_context(tc.psum_pool(name="psum_gates", bufs=PB))
-        psum_bias = ctx.enter_context(tc.psum_pool(name="psum_bias", bufs=BB))
+        psum_words = ctx.enter_context(tc.psum_pool(name="psum_words", bufs=5))
+        psum_gates = ctx.enter_context(tc.psum_pool(name="psum_gates", bufs=2))
+        psum_bias = ctx.enter_context(tc.psum_pool(name="psum_bias", bufs=1))
         ctx.enter_context(tc.manual_schedule())
 
         def gate_of(t):
@@ -70,11 +63,6 @@ def tile_yourlstm_pc_kernel(tc, h_below, gates_rec, c_old, w_ih, b_ih, b_hh, out
 
         bias_blocks = GATES * HIDDEN // P
         bias_rows = keep.tile([P, P], BF16)
-        filler_in = keep.tile([P, FILLER * PACK], BF16, align_bytes=64)
-        filler_codes = keep.tile([P, FILLER], U32, align_bytes=64)
-        filler_scales = keep.tile([P, FILLER], U8, align_bytes=64)
-        nc.vector.memset(filler_in[:], 1.0)
-        nc.vector.quantize_mx(out=filler_codes[:].bitcast(FP8X4), scales=filler_scales[:], in_=filler_in[:])
         nc.vector.memset(bias_rows[2 * bias_blocks : P, :], 0.0)
         nc.scalar.dma_start(out=bias_rows[0:bias_blocks, :], in_=b_ih.rearrange("(m r) -> m r", r=P))
         nc.scalar.dma_start(
@@ -157,13 +145,6 @@ def tile_yourlstm_pc_kernel(tc, h_below, gates_rec, c_old, w_ih, b_ih, b_hh, out
                     s == 0, s == PASSES - 1,
                 )
 
-        def fill(h, columns):
-            for i in range(columns // FILLER):
-                mx_pass(
-                    product_piece(h), filler_codes[:, 0:P], filler_scales[:, 0:P], filler_codes[:],
-                    filler_scales[:], True, True,
-                )
-
         def spread_biases(t):
             if t == 1:
                 bias_banks[t] = psum_gates.tile([P, BANK // P, P], F32, name="product", tag="product")
@@ -171,7 +152,7 @@ def tile_yourlstm_pc_kernel(tc, h_below, gates_rec, c_old, w_ih, b_ih, b_hh, out
                 bias_banks[t] = psum_bias.tile([P, BANK // P, P], F32, name="bias_bank", tag="bias_bank")
             for x in range(BANK // P):
                 m = (gate_of(t) * HIDDEN + part_of(t) * BANK) // P + x
-                if t < SUM_FROM:
+                if t in TURNED:
                     nc.tensor.transpose(bias_banks[t][:, x, :], bias_col[:, m : m + 1].to_broadcast([P, P]), ident_f32[:])
                 else:
                     nc.tensor.matmul(
@@ -181,7 +162,6 @@ def tile_yourlstm_pc_kernel(tc, h_below, gates_rec, c_old, w_ih, b_ih, b_hh, out
         def transpose(out, in_):
             nc.tensor.transpose(out, in_, ident_f32[:])
 
-        fill(0, FIRST)
         h_words = h_rows[:].bitcast(F32)
         h_t = psum_bias.tile([P, PASSES, HALVES, P], F32, tag="bias_bank")
         for s in range(PASSES):
@@ -197,7 +177,6 @@ def tile_yourlstm_pc_kernel(tc, h_below, gates_rec, c_old, w_ih, b_ih, b_hh, out
         h_scales = keep.tile([P, PASSES * P], U8, align_bytes=64)
         nc.vector.quantize_mx(out=h_codes[:].bitcast(FP8X4), scales=h_scales[:], in_=h_grouped[:])
 
-        fill(0, SECOND)
         bias_col = keep.tile([P, bias_blocks], F32)
 
         def transpose_biases():
@@ -280,7 +259,6 @@ def tile_yourlstm_pc_kernel(tc, h_below, gates_rec, c_old, w_ih, b_ih, b_hh, out
             tanh_c[part] = stage.tile([P, BANK], F32, name="tanh_c", tag="tanh_c")
             nc.scalar.activation(out=tanh_c[part][:], in_=c_new[:, units(part)], func=ACT.Tanh)
 
-        WHOLE = slice(0, BANK)
         for h in range(STEPS):
             t, e = divmod(h, PIECES)
             if h >= 3 and e == 0:
@@ -293,16 +271,13 @@ def tile_yourlstm_pc_kernel(tc, h_below, gates_rec, c_old, w_ih, b_ih, b_hh, out
             done = 0
             if h >= LAG:
                 multiply(h - LAG)
-                done += PASSES * ROWS
-            if e == 1 and SUM_FROM <= t + 1 < SLABS:
+            if e == 1 and len(TURNED) <= t + 1 < SLABS:
                 spread_biases(t + 1)
-                done += BANK
-            if h < STEPS - 1:
-                fill(max(h - LAG + 1, 0), BUSY - done)
-            if h == 0:
-                spread_biases(0)
-                spread_biases(1)
-                fill(0, BUSY)
+            elif LAG <= h < STEPS - 1:
+                multiply(h - LAG)
+            if h == 1:
+                for j in TURNED:
+                    spread_biases(j)
             for s in range(PASSES):
                 regroup(t, e, s)
             if h == 2:

@@ -273,8 +273,6 @@ def tile_yourlstm_pc_kernel(tc, h_below, gates_rec, c_old, w_ih, b_ih, b_hh, out
                 multiply(h - LAG)
             if e == 1 and len(TURNED) <= t + 1 < SLABS:
                 spread_biases(t + 1)
-            elif LAG <= h < STEPS - 1:
-                multiply(h - LAG)
             if h == 1:
                 for j in TURNED:
                     spread_biases(j)

from contextlib import ExitStack

import concourse.mybir as mybir
from concourse.masks import make_identity

F32 = mybir.dt.float32
BF16 = mybir.dt.bfloat16
U32 = mybir.dt.uint32
U8 = mybir.dt.uint8
FP8X4 = mybir.dt.float8_e4m3fn_x4
ACT = mybir.ActivationFunctionType
ALU = mybir.AluOpType

P = 128
FEATURES = 1024
HIDDEN = 1024
GATES = 4
GATE_F, GATE_G, GATE_O = 1, 2, 3
PACK = 4
PASSES = FEATURES // (P * PACK)
HALVES = 2
WORDS = FEATURES // 2
BANK = 512
PARTS = HIDDEN // BANK
SLABS = PARTS * GATES
PIECES = 2
ROWS = BANK // PIECES
TILES = ROWS // P
STEPS = SLABS * PIECES
WHOLE = slice(0, BANK)
TURNED = (0, 1)
LAG = 2
REC_AT = (1, 3)
C_AT = 2

FLOPS = 2 * P * FEATURES * GATES * HIDDEN


def tile_yourlstm_pc_kernel(tc, h_below, gates_rec, c_old, w_ih, b_ih, b_hh, out_0, out_1):
    nc = tc.nc
    with ExitStack() as ctx:
        keep = ctx.enter_context(tc.tile_pool(name="keep", bufs=1))
        w_pool = ctx.enter_context(tc.tile_pool(name="w", bufs=SLABS * PIECES))
        quant = ctx.enter_context(tc.tile_pool(name="quant", bufs=3 * PIECES))
        stage = ctx.enter_context(tc.tile_pool(name="stage", bufs=2))
        active_pool = ctx.enter_context(tc.tile_pool(name="active", bufs=GATES))
        psum_words = ctx.enter_context(tc.psum_pool(name="psum_words", bufs=5))
        psum_gates = ctx.enter_context(tc.psum_pool(name="psum_gates", bufs=2))
        psum_bias = ctx.enter_context(tc.psum_pool(name="psum_bias", bufs=1))
        ctx.enter_context(tc.manual_schedule())

        def gate_of(t):
            return t % GATE_O if t < PARTS * GATE_O else GATE_O

        def part_of(t):
            return t // GATE_O if t < PARTS * GATE_O else t - PARTS * GATE_O

        def live(t):
            return 0 <= t < SLABS

        def units(part):
            return slice(part * BANK, (part + 1) * BANK)

        bias_blocks = GATES * HIDDEN // P
        bias_rows = keep.tile([P, P], BF16)
        nc.vector.memset(bias_rows[2 * bias_blocks : P, :], 0.0)
        nc.scalar.dma_start(out=bias_rows[0:bias_blocks, :], in_=b_ih.rearrange("(m r) -> m r", r=P))
        nc.scalar.dma_start(
            out=bias_rows[bias_blocks : 2 * bias_blocks, :], in_=b_hh.rearrange("(m r) -> m r", r=P)
        )

        h_rows = keep.tile([P, FEATURES], BF16)
        nc.sync.dma_start(out=h_rows[:], in_=h_below)
        w_pieces = w_ih.rearrange("(g v e r x) k -> g v e r x k", g=GATES, v=PARTS, e=PIECES, r=P)
        rec_parts = gates_rec.rearrange("b (g v y) -> v b g y", g=GATES, v=PARTS)
        w_rows = {}
        rec_rows = {}
        c_rows = keep.tile([P, HIDDEN], BF16)
        for t in range(SLABS):
            for e in range(PIECES):
                w_rows[(t, e)] = w_pool.tile([P, TILES * FEATURES], BF16, name="w_rows", tag="w_rows")
                piece_rows = w_rows[(t, e)][:].rearrange("r (x k) -> r x k", x=TILES)
                source = w_pieces[gate_of(t), part_of(t), e]
                if (t, e) == (0, 0):
                    for x in range(TILES):
                        nc.sync.dma_start(out=piece_rows[:, x], in_=source[:, x])
                else:
                    nc.sync.dma_start(out=piece_rows, in_=source)
            if t in REC_AT:
                part = REC_AT.index(t)
                rec_rows[part] = keep.tile([P, GATES, BANK], BF16, name="rec_rows%d" % part)
                nc.sync.dma_start(out=rec_rows[part][:], in_=rec_parts[part])
            if t == C_AT:
                nc.sync.dma_start(out=c_rows[:], in_=c_old)

        ident_f32 = keep.tile([P, P], F32)
        make_identity(nc, ident_f32[:])
        ident_bf16 = keep.tile([P, P], BF16)
        nc.vector.tensor_copy(out=ident_bf16[:], in_=ident_f32[:])
        sel = keep.tile([P, bias_blocks], BF16)
        nc.vector.tensor_add(
            out=sel[:], in0=ident_bf16[:, 0:bias_blocks], in1=ident_bf16[:, bias_blocks : 2 * bias_blocks]
        )
        warm = keep.tile([P, 1], F32)
        nc.vector.memset(warm[:], 0.0)
        warm_out = keep.tile([P, 1], F32)
        nc.scalar.activation(out=warm_out[:], in_=warm[:], func=ACT.Sigmoid)

        c_new = keep.tile([P, HIDDEN], F32)
        h_new = keep.tile([P, HIDDEN], F32)
        bias_banks = {}
        rest = {}
        word_banks = {}
        grouped = {}
        codes = {}
        scales = {}
        products = {}
        gates = {}
        active = {}
        kept = {}
        fresh = {}
        tanh_c = {}

        def piece(e):
            return slice(e * ROWS, (e + 1) * ROWS)

        def product_piece(h):
            t, e = divmod(h, PIECES)
            if t not in products:
                products[t] = psum_gates.tile([P, BANK], F32, name="product", tag="product")
            return products[t][:, piece(e)]

        def mx_pass(out, lhs, lhs_scale, rhs, rhs_scale, start, stop):
            nc.tensor.matmul_mx(
                out=out, lhsT=lhs.bitcast(FP8X4), lhsT_scale=lhs_scale, rhs=rhs.bitcast(FP8X4), rhs_scale=rhs_scale,
                start=start, stop=stop,
            )

        def multiply(h):
            t, e = divmod(h, PIECES)
            for s in range(PASSES):
                mx_pass(
                    product_piece(h), h_codes[:, s * P : (s + 1) * P], h_scales[:, s * P : (s + 1) * P],
                    codes[(t, e)][:, s * ROWS : (s + 1) * ROWS], scales[(t, e)][:, s * ROWS : (s + 1) * ROWS],
                    s == 0, s == PASSES - 1,
                )

        def spread_biases(t):
            if t == 1:
                bias_banks[t] = psum_gates.tile([P, BANK // P, P], F32, name="product", tag="product")
            else:
                bias_banks[t] = psum_bias.tile([P, BANK // P, P], F32, name="bias_bank", tag="bias_bank")
            for x in range(BANK // P):
                m = (gate_of(t) * HIDDEN + part_of(t) * BANK) // P + x
                if t in TURNED:
                    nc.tensor.transpose(bias_banks[t][:, x, :], bias_col[:, m : m + 1].to_broadcast([P, P]), ident_f32[:])
                else:
                    nc.tensor.matmul(
                        bias_banks[t][:, x, :], sel[:, m : m + 1].to_broadcast([P, P]), bias_rows[:], start=True, stop=True
                    )

        def transpose(out, in_):
            nc.tensor.transpose(out, in_, ident_f32[:])

        h_words = h_rows[:].bitcast(F32)
        h_t = psum_bias.tile([P, PASSES, HALVES, P], F32, tag="bias_bank")
        for s in range(PASSES):
            for u in range(HALVES):
                first = s * HALVES * P
                transpose(h_t[:, s, u, :], h_words[:, first + u : first + HALVES * P : HALVES])
        h_grouped = keep.tile([P, PASSES * P * PACK], BF16, align_bytes=64)
        nc.vector.tensor_copy(
            out=h_grouped[:].bitcast(F32).rearrange("q (s m u) -> q s m u", s=PASSES, u=HALVES),
            in_=h_t[:].rearrange("q s u m -> q s m u"),
        )
        h_codes = keep.tile([P, PASSES * P], U32, align_bytes=64)
        h_scales = keep.tile([P, PASSES * P], U8, align_bytes=64)
        nc.vector.quantize_mx(out=h_codes[:].bitcast(FP8X4), scales=h_scales[:], in_=h_grouped[:])

        bias_col = keep.tile([P, bias_blocks], F32)

        def transpose_biases():
            bias_t = psum_bias.tile([P, P], BF16, tag="bias_bank")
            nc.tensor.transpose(bias_t[:], bias_rows[:], ident_bf16[:])
            bias_both = keep.tile([P, 2 * bias_blocks], F32)
            nc.vector.tensor_copy(out=bias_both[:], in_=bias_t[:, 0 : 2 * bias_blocks])
            nc.vector.tensor_add(
                out=bias_col[:], in0=bias_both[:, 0:bias_blocks], in1=bias_both[:, bias_blocks : 2 * bias_blocks]
            )

        def add_bias_to_rec(t):
            rest[t] = stage.tile([P, BANK], F32, name="rest", tag="rest")
            nc.vector.tensor_tensor(
                out=rest[t][:],
                in0=bias_banks[t][:].rearrange("b x r -> b (x r)"),
                in1=rec_rows[part_of(t)][:, gate_of(t), :],
                op=ALU.add,
            )

        def transpose_w(t, e, s, x):
            if (t, e, s) not in word_banks:
                word_banks[(t, e, s)] = psum_words.tile([P, TILES, HALVES, P], F32, name="word_bank", tag="word_bank")
            words = w_rows[(t, e)][:].bitcast(F32)
            for u in range(HALVES):
                first = x * WORDS + s * HALVES * P
                transpose(word_banks[(t, e, s)][:, x, u, :], words[:, first + u : first + HALVES * P : HALVES])

        def regroup(t, e, s):
            if s == 0:
                grouped[(t, e)] = quant.tile(
                    [P, PASSES * ROWS * PACK], BF16, name="grouped", tag="grouped", align_bytes=64
                )
            words = grouped[(t, e)][:].bitcast(F32)
            nc.scalar.copy(
                out=words[:, s * BANK : (s + 1) * BANK].rearrange("q (r x u) -> q r x u", x=TILES, u=HALVES),
                in_=word_banks[(t, e, s)][:].rearrange("q x u r -> q r x u"),
            )

        def quantise(t, e, first, last):
            if first == 0:
                codes[(t, e)] = quant.tile([P, PASSES * ROWS], U32, name="codes", tag="codes", align_bytes=64)
                scales[(t, e)] = quant.tile([P, PASSES * ROWS], U8, name="scales", tag="scales", align_bytes=64)
            cols = slice(first * ROWS, last * ROWS)
            nc.vector.quantize_mx(
                out=codes[(t, e)][:, cols].bitcast(FP8X4), scales=scales[(t, e)][:, cols],
                in_=grouped[(t, e)][:, first * ROWS * PACK : last * ROWS * PACK],
            )

        def add_rest(t, cols):
            if cols.start == 0:
                gates[t] = stage.tile([P, BANK], F32, name="gates", tag="gates")
                active[t] = active_pool.tile([P, BANK], F32, name="active", tag="active")
            nc.vector.tensor_tensor(out=gates[t][:, cols], in0=products[t][:, cols], in1=rest[t][:, cols], op=ALU.add)

        def activate(t, cols):
            func = ACT.Tanh if gate_of(t) == GATE_G else ACT.Sigmoid
            nc.scalar.activation(out=active[t][:, cols], in_=gates[t][:, cols], func=func)

        def emit_hidden(t, cols):
            part = part_of(t)
            out_cols = slice(part * BANK + cols.start, part * BANK + cols.stop)
            nc.vector.tensor_mul(out=h_new[:, out_cols], in0=active[t][:, cols], in1=tanh_c[part][:, cols])
            nc.sync.dma_start(out=out_0[:, out_cols], in_=h_new[:, out_cols])

        def use_gate(t):
            part = part_of(t)
            if gate_of(t) == GATE_F:
                kept[part] = stage.tile([P, BANK], F32, name="kept", tag="kept")
                nc.vector.tensor_mul(out=kept[part][:], in0=active[t][:], in1=c_rows[:, units(part)])
            if gate_of(t) == GATE_G:
                fresh[part] = stage.tile([P, BANK], F32, name="fresh", tag="fresh")
                nc.vector.tensor_mul(out=fresh[part][:], in0=active[t - GATE_G][:], in1=active[t][:])
                nc.vector.tensor_add(out=c_new[:, units(part)], in0=kept[part][:], in1=fresh[part][:])
                nc.sync.dma_start(out=out_1[:, units(part)], in_=c_new[:, units(part)])
            if gate_of(t) == GATE_O:
                emit_hidden(t, WHOLE)

        def activate_cell(part):
            tanh_c[part] = stage.tile([P, BANK], F32, name="tanh_c", tag="tanh_c")
            nc.scalar.activation(out=tanh_c[part][:], in_=c_new[:, units(part)], func=ACT.Tanh)

        for h in range(STEPS):
            t, e = divmod(h, PIECES)
            if h >= 3 and e == 0:
                add_bias_to_rec(t)
            for i in range(PASSES * TILES):
                s, x = divmod(i, TILES) if h else divmod(i, PASSES)[::-1]
                transpose_w(t, e, s, x)
            if h == 0:
                transpose_biases()
            done = 0
            if h >= LAG:
                multiply(h - LAG)
            if e == 1 and len(TURNED) <= t + 1 < SLABS:
                spread_biases(t + 1)
            if h == 1:
                for j in TURNED:
                    spread_biases(j)
            for s in range(PASSES):
                regroup(t, e, s)
            if h == 2:
                add_bias_to_rec(0)
                add_bias_to_rec(1)
            if e == 1:
                if t >= 1:
                    add_rest(t - 1, WHOLE)
                if t >= 2 and gate_of(t - 2) == GATE_G:
                    activate_cell(part_of(t - 2))
            elif t >= 2:
                activate(t - 2, WHOLE)
            if h < STEPS - 1:
                quantise(t, e, 0, PASSES)
            if e == 0 and t >= 2:
                use_gate(t - 2)
        multiply(h - 1)
        quantise(t, e, 0, 1)
        activate(t - 1, WHOLE)
        add_rest(t, piece(0))
        activate(t, piece(0))
        quantise(t, e, 1, 2)
        multiply(h)
        use_gate(t - 1)
        add_rest(t, piece(1))
        activate(t, piece(1))
        for e in range(PIECES):
            emit_hidden(t, piece(e))
